import numpy as np
import ml_dtypes


def mxq(x, axis, fmt="e4m3"):
    dtype, down = {"e4m3": (ml_dtypes.float8_e4m3fn, 7), "e5m2": (ml_dtypes.float8_e5m2, 14)}[fmt]
    v = np.moveaxis(np.asarray(x, np.float32).astype(ml_dtypes.bfloat16).astype(np.float64), axis, -1)
    blocks = v.reshape(v.shape[:-1] + (-1, 32))
    amax = np.abs(blocks).max(-1, keepdims=True)
    byte = np.maximum(np.where(amax > 0, np.frexp(amax)[1] - 1 + 127, 0) - down, 1)
    scale = np.exp2(byte - 127.0)
    codes = (blocks / scale).astype(np.float32).astype(dtype).astype(np.float64)
    return np.moveaxis((codes * scale).reshape(v.shape), -1, axis)


WIDE = False


def mx_kscale(k):
    if not WIDE:
        return np.ones(k)
    levels = np.array([10, -10, 5, -5, 0])
    a = np.random.permutation(np.resize(levels, k // 512 * 4)).reshape(k // 512, 4)
    idx = np.arange(k)
    return np.exp2(a[idx // 512, idx % 128 // 32])


BF16 = ml_dtypes.bfloat16


def bf(x):
    return np.asarray(x, np.float32).astype(BF16)


def f64(x):
    return np.asarray(x).astype(np.float64)


N, D, C, M = 14336, 512, 32, 4
LAMDA = 0.00390625
VS = 1.0 / (LAMDA * D)


def setup_inputs():
    s = mx_kscale(D)
    return {"x": bf(np.random.standard_normal((N, D)) * s),
            "x_var": bf(np.random.uniform(0.0, 1.0, (N, D)) * (0.5 + np.random.uniform(0.0, 1.0, (N, 1))) * 2.0 * VS),
            "proto_mean": bf(np.random.standard_normal((C, M, D)) / np.sqrt(D) / s),
            "proto_var": bf(np.random.uniform(0.0, 1.0, (C, M, D)) * (0.5 + np.random.uniform(0.0, 1.0, (C, M, 1))) * 2.0 * VS)}


def reference(x, x_var, proto_mean, proto_var):
    xv, pv = f64(x_var), f64(proto_var)
    dot = (mxq(f64(x), 1, "e4m3") @ mxq(f64(proto_mean), 2, "e4m3").reshape(C * M, D).T).reshape(N, C, M)
    cross = (mxq(np.sqrt(xv), 1, "e4m3") @ mxq(np.sqrt(pv), 2, "e4m3").reshape(C * M, D).T).reshape(N, C, M)
    var_term = xv.sum(-1)[:, None, None] + pv.sum(-1)[None, :, :] - 2.0 * cross
    return -(2.0 - 2.0 * dot + LAMDA * var_term)

@@ -1,0 +1,196 @@
+from contextlib import ExitStack
+
+import concourse.mybir as mybir
+from concourse.masks import make_identity
+
+F32 = mybir.dt.float32
+BF16 = mybir.dt.bfloat16
+U32 = mybir.dt.uint32
+U8 = mybir.dt.uint8
+FP8X4 = mybir.dt.float8_e4m3fn_x4
+ALU = mybir.AluOpType
+ACTF = mybir.ActivationFunctionType
+
+P = 128
+N_ROWS = 14336
+D = 512
+CM = 128
+LAMDA = 0.00390625
+T = 8
+N_CHUNKS = N_ROWS // (P * T)
+GROUPS_PER_CHUNK = T // 2
+N_GROUPS = N_CHUNKS * GROUPS_PER_CHUNK
+X_BUFS = 4
+
+FLOPS = 2 * 2 * N_ROWS * D * CM
+
+
+def tile_probprotoseghead_t_kernel(tc, x, x_var, proto_mean, proto_var, out):
+    nc = tc.nc
+    xc = x.rearrange("(c p t) d -> c p (t d)", p=P, t=T)
+    vc = x_var.rearrange("(c p t) d -> c p (t d)", p=P, t=T)
+    oc = out.rearrange("(c p t) a b -> c p (t a b)", p=P, t=T)
+
+    with ExitStack() as ctx:
+        ctx.enter_context(tc.manual_schedule())
+        consts = ctx.enter_context(tc.tile_pool(name="consts", bufs=1))
+        xpool = ctx.enter_context(tc.tile_pool(name="xpool", bufs=X_BUFS))
+        gpool = ctx.enter_context(tc.tile_pool(name="gpool", bufs=3))
+        cpool = ctx.enter_context(tc.tile_pool(name="cpool", bufs=3))
+        jpool = ctx.enter_context(tc.tile_pool(name="jpool", bufs=2))
+        opool = ctx.enter_context(tc.tile_pool(name="opool", bufs=3))
+        psum_t = ctx.enter_context(tc.psum_pool(name="psum_t", bufs=3))
+        psum_a = ctx.enter_context(tc.psum_pool(name="psum_a", bufs=2))
+
+        x_tiles = {}
+        v_tiles = {}
+
+        def load(c, cuts):
+            x_sb = xpool.tile([P, T * D], BF16, name="x_sb")
+            v_sb = xpool.tile([P, T * D], BF16, name="v_sb")
+            x_tiles[c] = x_sb
+            v_tiles[c] = v_sb
+            for lo, hi in cuts:
+                nc.sync.dma_start(out=x_sb[:, lo * D:hi * D], in_=xc[c][:, lo * D:hi * D])
+                nc.sync.dma_start(out=v_sb[:, lo * D:hi * D], in_=vc[c][:, lo * D:hi * D])
+
+        pm_sb = consts.tile([P, D], BF16)
+        pv_sb = consts.tile([P, D], BF16)
+        nc.scalar.dma_start(out=pm_sb[:], in_=proto_mean.rearrange("c m d -> (c m) d"))
+        nc.scalar.dma_start(out=pv_sb[:], in_=proto_var.rearrange("c m d -> (c m) d"))
+        load(0, [(0, 2), (2, T)])
+        for c in range(1, X_BUFS):
+            load(c, [(0, T)])
+
+        ident = consts.tile([P, P], F32)
+        make_identity(nc, ident[:])
+        warm_in = consts.tile([P, 1], F32)
+        warm_out = consts.tile([P, 1], F32)
+        nc.vector.memset(warm_in[:], 1.0)
+        nc.scalar.activation(out=warm_out[:], in_=warm_in[:], func=ACTF.Sqrt)
+        zeros = consts.tile([P, P], F32)
+        nc.vector.memset(zeros[:], 0.0)
+
+        s_all = consts.tile([P, N_GROUPS * 2], F32)
+        bias_cm = consts.tile([P, CM], F32)
+        p_grouped = consts.tile([P, 2 * 4 * CM], BF16, align_bytes=64)
+        p_codes = consts.tile([P, 2 * CM], U32, align_bytes=64)
+        p_plane = consts.tile([P, 2 * CM], U8, align_bytes=64)
+        p_sqrt = consts.tile([P, 4 * CM], F32)
+        sp_neg = consts.tile([P, 1], F32)
+        b_rep = consts.tile([P, P], F32)
+
+        pm_t = psum_t.tile([P, 2, 2 * P], F32, name="xt")
+        pv_t = psum_t.tile([P, 2, 2 * P], F32, name="vt")
+        for u in range(2):
+            nc.tensor.transpose(pm_t[:, u, 0:P], pm_sb[:].bitcast(F32)[:, u * P:(u + 1) * P], ident[:])
+        for u in range(2):
+            nc.tensor.transpose(pv_t[:, u, 0:P], pv_sb[:].bitcast(F32)[:, u * P:(u + 1) * P], ident[:])
+        nc.vector.tensor_scalar(
+            out=p_grouped[:, 0:4 * CM].rearrange("q (r u e) -> q r u e", u=2, e=2),
+            in0=pm_t[:].bitcast(BF16)[:, :, 0:2 * P].rearrange("q u (r e) -> q r u e", e=2),
+            scalar1=2.0, scalar2=None, op0=ALU.mult)
+        nc.scalar.activation(
+            out=p_sqrt[:].rearrange("q (r u e) -> q r u e", u=2, e=2),
+            in_=pv_t[:].bitcast(BF16)[:, :, 0:2 * P].rearrange("q u (r e) -> q r u e", e=2),
+            func=ACTF.Sqrt)
+        junk0 = jpool.tile([P, D], BF16, name="junk")
+        nc.vector.tensor_scalar(out=junk0[:], in0=pv_sb[:], scalar1=-LAMDA, scalar2=None,
+                                op0=ALU.mult, op1=ALU.add, accum_out=sp_neg[:])
+        nc.vector.tensor_scalar(out=b_rep[:], in0=zeros[:], scalar1=sp_neg[:, 0:1], scalar2=-2.0,
+                                op0=ALU.add, op1=ALU.add)
+        nc.vector.tensor_scalar(out=p_grouped[:, 4 * CM:8 * CM], in0=p_sqrt[:],
+                                scalar1=2.0 * LAMDA, scalar2=None, op0=ALU.mult)
+        nc.vector.quantize_mx(out=p_codes[:].bitcast(FP8X4), scales=p_plane[:], in_=p_grouped[:])
+        b_t = psum_a.tile([P, 2, P], F32, name="acc")
+        nc.tensor.transpose(b_t[:, 0, :], b_rep[:], ident[:])
+        nc.vector.tensor_copy(out=bias_cm[:], in_=b_t[:, 0, :])
+
+        banks = {}
+        grouped = {}
+        codes = {}
+        accs = {}
+        o_tiles = {}
+
+        def where(g):
+            return g // GROUPS_PER_CHUNK, 2 * (g % GROUPS_PER_CHUNK)
+
+        def transposes(g):
+            c, t0 = where(g)
+            xt = psum_t.tile([P, 2, 2 * P], F32, name="xt")
+            vt = psum_t.tile([P, 2, 2 * P], F32, name="vt")
+            banks[g] = (xt, vt)
+            for src, dst in ((x_tiles[c], xt), (v_tiles[c], vt)):
+                words = src[:].bitcast(F32)
+                for u in range(2):
+                    for j in range(2):
+                        w0 = (t0 + j) * (D // 2) + u * P
+                        nc.tensor.transpose(dst[:, u, j * P:(j + 1) * P], words[:, w0:w0 + P], ident[:])
+
+        def evacuate(g):
+            xt, vt = banks[g]
+            gr = gpool.tile([P, 2048], BF16, name="gr", align_bytes=64)
+            grouped[g] = gr
+            nc.scalar.copy(out=gr[:, 0:1024].bitcast(F32).rearrange("q (n u) -> q n u", u=2),
+                           in_=xt[:].rearrange("q u n -> q n u"))
+            nc.scalar.activation(out=gr[:, 1024:2048].rearrange("q (n u e) -> q n u e", u=2, e=2),
+                                 in_=vt[:].bitcast(BF16).rearrange("q u (n e) -> q n u e", e=2),
+                                 func=ACTF.Sqrt)
+
+        def quantise(g):
+            gr = grouped[g]
+            cd = cpool.tile([P, 512], U32, name="cd", align_bytes=64)
+            pl = cpool.tile([P, 512], U8, name="pl", align_bytes=64)
+            codes[g] = (cd, pl)
+            nc.vector.quantize_mx(out=cd[:].bitcast(FP8X4), scales=pl[:], in_=gr[:])
+
+        def multiply(g):
+            cd, pl = codes[g]
+            acc = psum_a.tile([P, 2, P], F32, name="acc")
+            accs[g] = acc
+            for j in range(2):
+                for h in range(2):
+                    cols = slice(h * 256 + j * P, h * 256 + (j + 1) * P)
+                    pcols = slice(h * CM, (h + 1) * CM)
+                    nc.tensor.matmul_mx(out=acc[:, j, :],
+                                        lhsT=cd[:, cols].bitcast(FP8X4), lhsT_scale=pl[:, cols],
+                                        rhs=p_codes[:, pcols].bitcast(FP8X4), rhs_scale=p_plane[:, pcols],
+                                        start=(h == 0), stop=(h == 1))
+
+        def row_sums(g):
+            c, t0 = where(g)
+            for j in range(2):
+                junk = jpool.tile([P, D], BF16, name="junk")
+                nc.vector.tensor_scalar(out=junk[:], in0=v_tiles[c][:, (t0 + j) * D:(t0 + j + 1) * D],
+                                        scalar1=-LAMDA, scalar2=None, op0=ALU.mult, op1=ALU.add,
+                                        accum_out=s_all[:, 2 * g + j:2 * g + j + 1])
+
+        def combine(g):
+            c, t0 = where(g)
+            acc = accs[g]
+            if t0 == 0:
+                o_tiles[c] = opool.tile([P, T * CM], F32, name="o_sb")
+            o_sb = o_tiles[c]
+            for j in range(2):
+                nc.vector.scalar_tensor_tensor(out=o_sb[:, (t0 + j) * CM:(t0 + j + 1) * CM],
+                                               in0=acc[:, j, :], scalar=s_all[:, 2 * g + j:2 * g + j + 1],
+                                               in1=bias_cm[:], op0=ALU.add, op1=ALU.add)
+            if c == N_CHUNKS - 1:
+                nc.sync.dma_start(out=oc[c][:, t0 * CM:(t0 + 2) * CM], in_=o_sb[:, t0 * CM:(t0 + 2) * CM])
+            elif t0 == T - 2:
+                nc.sync.dma_start(out=oc[c], in_=o_sb[:])
+
+        for i in range(N_GROUPS + 3):
+            if i < N_GROUPS:
+                transposes(i)
+                evacuate(i)
+            if 0 <= i - 2 < N_GROUPS:
+                quantise(i - 2)
+                multiply(i - 2)
+            if 0 <= i - 3 < N_GROUPS:
+                combine(i - 3)
+            if i < N_GROUPS:
+                row_sums(i)
+                c, t0 = where(i)
+                if t0 == T - 2 and c + X_BUFS < N_CHUNKS:
+                    load(c + X_BUFS, [(0, T)])

@@ -21,6 +21,12 @@ N_CHUNKS = N_ROWS // (P * T)
 GROUPS_PER_CHUNK = T // 2
 N_GROUPS = N_CHUNKS * GROUPS_PER_CHUNK
 X_BUFS = 4
+S_COLS = 128
+
+
+def pe_sums(g):
+    return g % 5 == 2
+
 
 FLOPS = 2 * 2 * N_ROWS * D * CM
 
@@ -74,6 +80,7 @@ def tile_probprotoseghead_t_kernel(tc, x, x_var, proto_mean, proto_var, out):
         s_all = consts.tile([P, N_GROUPS * 2], F32)
         bias_cm = consts.tile([P, CM], F32)
         p_grouped = consts.tile([P, 2 * 4 * CM], BF16, align_bytes=64)
+        neg_ident = consts.tile([P, P], BF16)
         p_codes = consts.tile([P, 2 * CM], U32, align_bytes=64)
         p_plane = consts.tile([P, 2 * CM], U8, align_bytes=64)
         p_sqrt = consts.tile([P, 4 * CM], F32)
@@ -102,7 +109,8 @@ def tile_probprotoseghead_t_kernel(tc, x, x_var, proto_mean, proto_var, out):
         nc.vector.tensor_scalar(out=p_grouped[:, 4 * CM:8 * CM], in0=p_sqrt[:],
                                 scalar1=2.0 * LAMDA, scalar2=None, op0=ALU.mult)
         nc.vector.quantize_mx(out=p_codes[:].bitcast(FP8X4), scales=p_plane[:], in_=p_grouped[:])
-        b_t = psum_a.tile([P, 2, P], F32, name="acc")
+        nc.vector.tensor_scalar(out=neg_ident[:], in0=ident[:], scalar1=-LAMDA, scalar2=None, op0=ALU.mult)
+        b_t = psum_a.tile([P, 4, P], F32, name="acc")
         nc.tensor.transpose(b_t[:, 0, :], b_rep[:], ident[:])
         nc.vector.tensor_copy(out=bias_cm[:], in_=b_t[:, 0, :])
 
@@ -146,8 +154,7 @@ def tile_probprotoseghead_t_kernel(tc, x, x_var, proto_mean, proto_var, out):
 
         def multiply(g):
             cd, pl = codes[g]
-            acc = psum_a.tile([P, 2, P], F32, name="acc")
-            accs[g] = acc
+            acc = accs[g]
             for j in range(2):
                 for h in range(2):
                     cols = slice(h * 256 + j * P, h * 256 + (j + 1) * P)
@@ -164,6 +171,19 @@ def tile_probprotoseghead_t_kernel(tc, x, x_var, proto_mean, proto_var, out):
                 nc.vector.tensor_scalar(out=junk[:], in0=v_tiles[c][:, (t0 + j) * D:(t0 + j + 1) * D],
                                         scalar1=-LAMDA, scalar2=None, op0=ALU.mult, op1=ALU.add,
                                         accum_out=s_all[:, 2 * g + j:2 * g + j + 1])
+
+        def matmul_sums(g):
+            c, t0 = where(g)
+            parts = D // S_COLS
+            for j in range(2):
+                for u in range(parts):
+                    lo = (t0 + j) * D + u * S_COLS
+                    nc.tensor.matmul(out=accs[g][:, 2 + j, :], lhsT=neg_ident[:], rhs=v_tiles[c][:, lo:lo + S_COLS],
+                                     start=(u == 0), stop=(u == parts - 1))
+
+        def reduce_sums(g):
+            nc.vector.tensor_reduce(out=s_all[:, 2 * g:2 * g + 2], in_=accs[g][:, 2:4, :],
+                                    axis=mybir.AxisListType.X, op=ALU.add)
 
         def combine(g):
             c, t0 = where(g)
@@ -184,13 +204,19 @@ def tile_probprotoseghead_t_kernel(tc, x, x_var, proto_mean, proto_var, out):
             if i < N_GROUPS:
                 transposes(i)
                 evacuate(i)
+            if 0 <= i - 3 < N_GROUPS and pe_sums(i - 3):
+                reduce_sums(i - 3)
             if 0 <= i - 2 < N_GROUPS:
+                accs[i - 2] = psum_a.tile([P, 4, P], F32, name="acc")
+                if pe_sums(i - 2):
+                    matmul_sums(i - 2)
                 quantise(i - 2)
                 multiply(i - 2)
             if 0 <= i - 3 < N_GROUPS:
                 combine(i - 3)
             if i < N_GROUPS:
-                row_sums(i)
+                if not pe_sums(i):
+                    row_sums(i)
                 c, t0 = where(i)
                 if t0 == T - 2 and c + X_BUFS < N_CHUNKS:
                     load(c + X_BUFS, [(0, T)])

@@ -25,7 +25,15 @@ S_COLS = 128
 
 
 def pe_sums(g):
-    return g % 5 == 2
+    return g % 5 in (0, 3) and g > 0
+
+
+def vector_x(g):
+    return g % 20 == 15
+
+
+def split(g):
+    return g == N_GROUPS - 1
 
 
 FLOPS = 2 * 2 * N_ROWS * D * CM
@@ -41,7 +49,7 @@ def tile_probprotoseghead_t_kernel(tc, x, x_var, proto_mean, proto_var, out):
         ctx.enter_context(tc.manual_schedule())
         consts = ctx.enter_context(tc.tile_pool(name="consts", bufs=1))
         xpool = ctx.enter_context(tc.tile_pool(name="xpool", bufs=X_BUFS))
-        gpool = ctx.enter_context(tc.tile_pool(name="gpool", bufs=3))
+        gpool = ctx.enter_context(tc.tile_pool(name="gpool", bufs=5))
         cpool = ctx.enter_context(tc.tile_pool(name="cpool", bufs=3))
         jpool = ctx.enter_context(tc.tile_pool(name="jpool", bufs=2))
         opool = ctx.enter_context(tc.tile_pool(name="opool", bufs=3))
@@ -64,8 +72,9 @@ def tile_probprotoseghead_t_kernel(tc, x, x_var, proto_mean, proto_var, out):
         pv_sb = consts.tile([P, D], BF16)
         nc.scalar.dma_start(out=pm_sb[:], in_=proto_mean.rearrange("c m d -> (c m) d"))
         nc.scalar.dma_start(out=pv_sb[:], in_=proto_var.rearrange("c m d -> (c m) d"))
-        load(0, [(0, 2), (2, T)])
-        for c in range(1, X_BUFS):
+        load(0, [(0, 2), (2, 4), (4, T)])
+        load(1, [(0, 4), (4, T)])
+        for c in range(2, X_BUFS):
             load(c, [(0, T)])
 
         ident = consts.tile([P, P], F32)
@@ -87,38 +96,41 @@ def tile_probprotoseghead_t_kernel(tc, x, x_var, proto_mean, proto_var, out):
         sp_neg = consts.tile([P, 1], F32)
         b_rep = consts.tile([P, P], F32)
 
-        pm_t = psum_t.tile([P, 2, 2 * P], F32, name="xt")
-        pv_t = psum_t.tile([P, 2, 2 * P], F32, name="vt")
-        for u in range(2):
-            nc.tensor.transpose(pm_t[:, u, 0:P], pm_sb[:].bitcast(F32)[:, u * P:(u + 1) * P], ident[:])
-        for u in range(2):
-            nc.tensor.transpose(pv_t[:, u, 0:P], pv_sb[:].bitcast(F32)[:, u * P:(u + 1) * P], ident[:])
-        nc.vector.tensor_scalar(
-            out=p_grouped[:, 0:4 * CM].rearrange("q (r u e) -> q r u e", u=2, e=2),
-            in0=pm_t[:].bitcast(BF16)[:, :, 0:2 * P].rearrange("q u (r e) -> q r u e", e=2),
-            scalar1=2.0, scalar2=None, op0=ALU.mult)
-        nc.scalar.activation(
-            out=p_sqrt[:].rearrange("q (r u e) -> q r u e", u=2, e=2),
-            in_=pv_t[:].bitcast(BF16)[:, :, 0:2 * P].rearrange("q u (r e) -> q r u e", e=2),
-            func=ACTF.Sqrt)
-        junk0 = jpool.tile([P, D], BF16, name="junk")
-        nc.vector.tensor_scalar(out=junk0[:], in0=pv_sb[:], scalar1=-LAMDA, scalar2=None,
-                                op0=ALU.mult, op1=ALU.add, accum_out=sp_neg[:])
-        nc.vector.tensor_scalar(out=b_rep[:], in0=zeros[:], scalar1=sp_neg[:, 0:1], scalar2=-2.0,
-                                op0=ALU.add, op1=ALU.add)
-        nc.vector.tensor_scalar(out=p_grouped[:, 4 * CM:8 * CM], in0=p_sqrt[:],
-                                scalar1=2.0 * LAMDA, scalar2=None, op0=ALU.mult)
-        nc.vector.quantize_mx(out=p_codes[:].bitcast(FP8X4), scales=p_plane[:], in_=p_grouped[:])
-        nc.vector.tensor_scalar(out=neg_ident[:], in0=ident[:], scalar1=-LAMDA, scalar2=None, op0=ALU.mult)
-        b_t = psum_a.tile([P, 4, P], F32, name="acc")
-        nc.tensor.transpose(b_t[:, 0, :], b_rep[:], ident[:])
-        nc.vector.tensor_copy(out=bias_cm[:], in_=b_t[:, 0, :])
-
         banks = {}
         grouped = {}
         codes = {}
         accs = {}
         o_tiles = {}
+
+        def prototypes():
+            pm_t = psum_t.tile([P, 2, 2 * P], F32, name="xt")
+            pv_t = psum_t.tile([P, 2, 2 * P], F32, name="vt")
+            for u in range(2):
+                nc.tensor.transpose(pm_t[:, u, 0:P], pm_sb[:].bitcast(F32)[:, u * P:(u + 1) * P], ident[:])
+            for u in range(2):
+                nc.tensor.transpose(pv_t[:, u, 0:P], pv_sb[:].bitcast(F32)[:, u * P:(u + 1) * P], ident[:])
+            nc.vector.tensor_scalar(
+                out=p_grouped[:, 0:4 * CM].rearrange("q (r u e) -> q r u e", u=2, e=2),
+                in0=pm_t[:].bitcast(BF16)[:, :, 0:2 * P].rearrange("q u (r e) -> q r u e", e=2),
+                scalar1=2.0, scalar2=None, op0=ALU.mult)
+            nc.scalar.activation(
+                out=p_sqrt[:].rearrange("q (r u e) -> q r u e", u=2, e=2),
+                in_=pv_t[:].bitcast(BF16)[:, :, 0:2 * P].rearrange("q u (r e) -> q r u e", e=2),
+                func=ACTF.Sqrt)
+            junk0 = jpool.tile([P, D], BF16, name="junk")
+            nc.vector.tensor_scalar(out=junk0[:], in0=pv_sb[:], scalar1=-LAMDA, scalar2=None,
+                                    op0=ALU.mult, op1=ALU.add, accum_out=sp_neg[:])
+            nc.vector.tensor_scalar(out=b_rep[:], in0=zeros[:], scalar1=sp_neg[:, 0:1], scalar2=-2.0,
+                                    op0=ALU.add, op1=ALU.add)
+            nc.vector.tensor_scalar(out=p_grouped[:, 4 * CM:8 * CM], in0=p_sqrt[:],
+                                    scalar1=2.0 * LAMDA, scalar2=None, op0=ALU.mult)
+            nc.vector.quantize_mx(out=p_codes[:].bitcast(FP8X4), scales=p_plane[:], in_=p_grouped[:])
+            nc.vector.tensor_scalar(out=neg_ident[:], in0=ident[:], scalar1=-LAMDA, scalar2=None, op0=ALU.mult)
+
+        def bias_row():
+            b_t = psum_a.tile([P, 4, P], F32, name="acc")
+            nc.tensor.transpose(b_t[:, 0, :], b_rep[:], ident[:])
+            nc.vector.tensor_copy(out=bias_cm[:], in_=b_t[:, 0, :])
 
         def where(g):
             return g // GROUPS_PER_CHUNK, 2 * (g % GROUPS_PER_CHUNK)
@@ -135,29 +147,42 @@ def tile_probprotoseghead_t_kernel(tc, x, x_var, proto_mean, proto_var, out):
                         w0 = (t0 + j) * (D // 2) + u * P
                         nc.tensor.transpose(dst[:, u, j * P:(j + 1) * P], words[:, w0:w0 + P], ident[:])
 
-        def evacuate(g):
-            xt, vt = banks[g]
-            gr = gpool.tile([P, 2048], BF16, name="gr", align_bytes=64)
-            grouped[g] = gr
-            nc.scalar.copy(out=gr[:, 0:1024].bitcast(F32).rearrange("q (n u) -> q n u", u=2),
-                           in_=xt[:].rearrange("q u n -> q n u"))
-            nc.scalar.activation(out=gr[:, 1024:2048].rearrange("q (n u e) -> q n u e", u=2, e=2),
-                                 in_=vt[:].bitcast(BF16).rearrange("q u (n e) -> q n u e", e=2),
-                                 func=ACTF.Sqrt)
+        def parts_x(g):
+            return [(0, P, 0, 512), (P, 2 * P, 1024, 1536)] if split(g) else [(0, 2 * P, 0, 1024)]
+
+        def parts_v(g):
+            return [(0, P, 512, 1024), (P, 2 * P, 1536, 2048)] if split(g) else [(0, 2 * P, 1024, 2048)]
+
+        def evacuate_x(g):
+            copy = nc.vector.tensor_copy if vector_x(g) else nc.scalar.copy
+            src = banks[g][0][:].rearrange("q u n -> q n u")
+            for n0, n1, lo, hi in parts_x(g):
+                copy(out=grouped[g][:, lo:hi].bitcast(F32).rearrange("q (n u) -> q n u", u=2), in_=src[:, n0:n1, :])
+
+        def evacuate_v(g):
+            src = banks[g][1][:].bitcast(BF16).rearrange("q u (n e) -> q n u e", e=2)
+            for n0, n1, lo, hi in parts_v(g):
+                nc.scalar.activation(out=grouped[g][:, lo:hi].rearrange("q (n u e) -> q n u e", u=2, e=2),
+                                     in_=src[:, n0:n1, :, :], func=ACTF.Sqrt)
 
         def quantise(g):
             gr = grouped[g]
             cd = cpool.tile([P, 512], U32, name="cd", align_bytes=64)
             pl = cpool.tile([P, 512], U8, name="pl", align_bytes=64)
             codes[g] = (cd, pl)
-            nc.vector.quantize_mx(out=cd[:].bitcast(FP8X4), scales=pl[:], in_=gr[:])
+            for j in range(2 if split(g) else 1):
+                n = 256 if split(g) else 512
+                cols = slice(j * n, (j + 1) * n)
+                nc.vector.quantize_mx(out=cd[:, cols].bitcast(FP8X4), scales=pl[:, cols],
+                                      in_=gr[:, 4 * j * n:4 * (j + 1) * n])
 
         def multiply(g):
             cd, pl = codes[g]
             acc = accs[g]
             for j in range(2):
                 for h in range(2):
-                    cols = slice(h * 256 + j * P, h * 256 + (j + 1) * P)
+                    lo = (2 * j + h) * P if split(g) else (2 * h + j) * P
+                    cols = slice(lo, lo + P)
                     pcols = slice(h * CM, (h + 1) * CM)
                     nc.tensor.matmul_mx(out=acc[:, j, :],
                                         lhsT=cd[:, cols].bitcast(FP8X4), lhsT_scale=pl[:, cols],
@@ -167,6 +192,8 @@ def tile_probprotoseghead_t_kernel(tc, x, x_var, proto_mean, proto_var, out):
         def row_sums(g):
             c, t0 = where(g)
             for j in range(2):
+                if j == 0 and pe_sums(g):
+                    continue
                 junk = jpool.tile([P, D], BF16, name="junk")
                 nc.vector.tensor_scalar(out=junk[:], in0=v_tiles[c][:, (t0 + j) * D:(t0 + j + 1) * D],
                                         scalar1=-LAMDA, scalar2=None, op0=ALU.mult, op1=ALU.add,
@@ -175,14 +202,13 @@ def tile_probprotoseghead_t_kernel(tc, x, x_var, proto_mean, proto_var, out):
         def matmul_sums(g):
             c, t0 = where(g)
             parts = D // S_COLS
-            for j in range(2):
-                for u in range(parts):
-                    lo = (t0 + j) * D + u * S_COLS
-                    nc.tensor.matmul(out=accs[g][:, 2 + j, :], lhsT=neg_ident[:], rhs=v_tiles[c][:, lo:lo + S_COLS],
-                                     start=(u == 0), stop=(u == parts - 1))
+            for u in range(parts):
+                lo = t0 * D + u * S_COLS
+                nc.tensor.matmul(out=accs[g][:, 2, :], lhsT=neg_ident[:], rhs=v_tiles[c][:, lo:lo + S_COLS],
+                                 start=(u == 0), stop=(u == parts - 1))
 
         def reduce_sums(g):
-            nc.vector.tensor_reduce(out=s_all[:, 2 * g:2 * g + 2], in_=accs[g][:, 2:4, :],
+            nc.vector.tensor_reduce(out=s_all[:, 2 * g:2 * g + 1], in_=accs[g][:, 2, :],
                                     axis=mybir.AxisListType.X, op=ALU.add)
 
         def combine(g):
@@ -201,22 +227,34 @@ def tile_probprotoseghead_t_kernel(tc, x, x_var, proto_mean, proto_var, out):
                 nc.sync.dma_start(out=oc[c], in_=o_sb[:])
 
         for i in range(N_GROUPS + 3):
+            q = i - 2
             if i < N_GROUPS:
                 transposes(i)
-                evacuate(i)
-            if 0 <= i - 3 < N_GROUPS and pe_sums(i - 3):
-                reduce_sums(i - 3)
-            if 0 <= i - 2 < N_GROUPS:
-                accs[i - 2] = psum_a.tile([P, 4, P], F32, name="acc")
-                if pe_sums(i - 2):
-                    matmul_sums(i - 2)
-                quantise(i - 2)
-                multiply(i - 2)
-            if 0 <= i - 3 < N_GROUPS:
-                combine(i - 3)
+                grouped[i] = gpool.tile([P, 2048], BF16, name="gr", align_bytes=64)
+                if not vector_x(i):
+                    evacuate_x(i)
+                evacuate_v(i)
+            if 0 <= q < N_GROUPS:
+                accs[q] = psum_a.tile([P, 4, P], F32, name="acc")
+            if 0 <= q < N_GROUPS and pe_sums(q):
+                matmul_sums(q)
+            if 0 <= q < N_GROUPS:
+                quantise(q)
+            if 0 <= q < N_GROUPS:
+                multiply(q)
+            if 0 <= q - 1 < N_GROUPS:
+                combine(q - 1)
+            if 0 <= q < N_GROUPS and pe_sums(q):
+                reduce_sums(q)
+            if 0 <= i - 0 < N_GROUPS and vector_x(i - 0):
+                evacuate_x(i - 0)
+            if 0 <= i + 0 < N_GROUPS:
+                row_sums(i + 0)
+            if i == 0:
+                prototypes()
+            if i == 1:
+                bias_row()
             if i < N_GROUPS:
-                if not pe_sums(i):
-                    row_sums(i)
                 c, t0 = where(i)
                 if t0 == T - 2 and c + X_BUFS < N_CHUNKS:
                     load(c + X_BUFS, [(0, T)])

@@ -25,15 +25,19 @@ S_COLS = 128
 
 
 def pe_sums(g):
-    return g % 5 in (0, 3) and g > 0
+    return g % 5 in (1, 4)
+
+
+def raw_v(g):
+    return False
 
 
 def vector_x(g):
-    return g % 20 == 15
+    return g % 11 == 5
 
 
-def split(g):
-    return g == N_GROUPS - 1
+def vector_raw(g):
+    return False
 
 
 FLOPS = 2 * 2 * N_ROWS * D * CM
@@ -49,9 +53,10 @@ def tile_probprotoseghead_t_kernel(tc, x, x_var, proto_mean, proto_var, out):
         ctx.enter_context(tc.manual_schedule())
         consts = ctx.enter_context(tc.tile_pool(name="consts", bufs=1))
         xpool = ctx.enter_context(tc.tile_pool(name="xpool", bufs=X_BUFS))
-        gpool = ctx.enter_context(tc.tile_pool(name="gpool", bufs=5))
-        cpool = ctx.enter_context(tc.tile_pool(name="cpool", bufs=3))
+        gpool = ctx.enter_context(tc.tile_pool(name="gpool", bufs=6))
+        cpool = ctx.enter_context(tc.tile_pool(name="cpool", bufs=5))
         jpool = ctx.enter_context(tc.tile_pool(name="jpool", bufs=2))
+        rpool = ctx.enter_context(tc.tile_pool(name="rpool", bufs=2))
         opool = ctx.enter_context(tc.tile_pool(name="opool", bufs=3))
         psum_t = ctx.enter_context(tc.psum_pool(name="psum_t", bufs=3))
         psum_a = ctx.enter_context(tc.psum_pool(name="psum_a", bufs=2))
@@ -89,6 +94,8 @@ def tile_probprotoseghead_t_kernel(tc, x, x_var, proto_mean, proto_var, out):
         s_all = consts.tile([P, N_GROUPS * 2], F32)
         bias_cm = consts.tile([P, CM], F32)
         p_grouped = consts.tile([P, 2 * 4 * CM], BF16, align_bytes=64)
+        neg_col = consts.tile([P, 1], BF16)
+        nc.vector.memset(neg_col[:], -LAMDA)
         neg_ident = consts.tile([P, P], BF16)
         p_codes = consts.tile([P, 2 * CM], U32, align_bytes=64)
         p_plane = consts.tile([P, 2 * CM], U8, align_bytes=64)
@@ -100,6 +107,7 @@ def tile_probprotoseghead_t_kernel(tc, x, x_var, proto_mean, proto_var, out):
         grouped = {}
         codes = {}
         accs = {}
+        raws = {}
         o_tiles = {}
 
         def prototypes():
@@ -120,10 +128,14 @@ def tile_probprotoseghead_t_kernel(tc, x, x_var, proto_mean, proto_var, out):
             junk0 = jpool.tile([P, D], BF16, name="junk")
             nc.vector.tensor_scalar(out=junk0[:], in0=pv_sb[:], scalar1=-LAMDA, scalar2=None,
                                     op0=ALU.mult, op1=ALU.add, accum_out=sp_neg[:])
+
+        def prototypes_scale():
             nc.vector.tensor_scalar(out=b_rep[:], in0=zeros[:], scalar1=sp_neg[:, 0:1], scalar2=-2.0,
                                     op0=ALU.add, op1=ALU.add)
             nc.vector.tensor_scalar(out=p_grouped[:, 4 * CM:8 * CM], in0=p_sqrt[:],
                                     scalar1=2.0 * LAMDA, scalar2=None, op0=ALU.mult)
+
+        def prototypes_quantise():
             nc.vector.quantize_mx(out=p_codes[:].bitcast(FP8X4), scales=p_plane[:], in_=p_grouped[:])
             nc.vector.tensor_scalar(out=neg_ident[:], in0=ident[:], scalar1=-LAMDA, scalar2=None, op0=ALU.mult)
 
@@ -147,42 +159,35 @@ def tile_probprotoseghead_t_kernel(tc, x, x_var, proto_mean, proto_var, out):
                         w0 = (t0 + j) * (D // 2) + u * P
                         nc.tensor.transpose(dst[:, u, j * P:(j + 1) * P], words[:, w0:w0 + P], ident[:])
 
-        def parts_x(g):
-            return [(0, P, 0, 512), (P, 2 * P, 1024, 1536)] if split(g) else [(0, 2 * P, 0, 1024)]
-
-        def parts_v(g):
-            return [(0, P, 512, 1024), (P, 2 * P, 1536, 2048)] if split(g) else [(0, 2 * P, 1024, 2048)]
-
         def evacuate_x(g):
-            copy = nc.vector.tensor_copy if vector_x(g) else nc.scalar.copy
+            dst = grouped[g][:, 0:1024].bitcast(F32).rearrange("q (n u) -> q n u", u=2)
             src = banks[g][0][:].rearrange("q u n -> q n u")
-            for n0, n1, lo, hi in parts_x(g):
-                copy(out=grouped[g][:, lo:hi].bitcast(F32).rearrange("q (n u) -> q n u", u=2), in_=src[:, n0:n1, :])
+            if vector_x(g):
+                nc.vector.tensor_copy(out=dst, in_=src)
+            else:
+                nc.scalar.copy(out=dst, in_=src)
 
         def evacuate_v(g):
-            src = banks[g][1][:].bitcast(BF16).rearrange("q u (n e) -> q n u e", e=2)
-            for n0, n1, lo, hi in parts_v(g):
-                nc.scalar.activation(out=grouped[g][:, lo:hi].rearrange("q (n u e) -> q n u e", u=2, e=2),
-                                     in_=src[:, n0:n1, :, :], func=ACTF.Sqrt)
+            vt = banks[g][1]
+            gr = grouped[g]
+            src = raws[g] if raw_v(g) else vt
+            nc.scalar.activation(out=gr[:, 1024:2048].rearrange("q (n u e) -> q n u e", u=2, e=2),
+                                 in_=src[:].bitcast(BF16).rearrange("q u (n e) -> q n u e", e=2),
+                                 func=ACTF.Sqrt)
 
         def quantise(g):
             gr = grouped[g]
             cd = cpool.tile([P, 512], U32, name="cd", align_bytes=64)
             pl = cpool.tile([P, 512], U8, name="pl", align_bytes=64)
             codes[g] = (cd, pl)
-            for j in range(2 if split(g) else 1):
-                n = 256 if split(g) else 512
-                cols = slice(j * n, (j + 1) * n)
-                nc.vector.quantize_mx(out=cd[:, cols].bitcast(FP8X4), scales=pl[:, cols],
-                                      in_=gr[:, 4 * j * n:4 * (j + 1) * n])
+            nc.vector.quantize_mx(out=cd[:].bitcast(FP8X4), scales=pl[:], in_=gr[:])
 
         def multiply(g):
             cd, pl = codes[g]
             acc = accs[g]
             for j in range(2):
                 for h in range(2):
-                    lo = (2 * j + h) * P if split(g) else (2 * h + j) * P
-                    cols = slice(lo, lo + P)
+                    cols = slice(h * 256 + j * P, h * 256 + (j + 1) * P)
                     pcols = slice(h * CM, (h + 1) * CM)
                     nc.tensor.matmul_mx(out=acc[:, j, :],
                                         lhsT=cd[:, cols].bitcast(FP8X4), lhsT_scale=pl[:, cols],
@@ -192,7 +197,7 @@ def tile_probprotoseghead_t_kernel(tc, x, x_var, proto_mean, proto_var, out):
         def row_sums(g):
             c, t0 = where(g)
             for j in range(2):
-                if j == 0 and pe_sums(g):
+                if raw_v(g) or (j == 0 and pe_sums(g)):
                     continue
                 junk = jpool.tile([P, D], BF16, name="junk")
                 nc.vector.tensor_scalar(out=junk[:], in0=v_tiles[c][:, (t0 + j) * D:(t0 + j + 1) * D],
@@ -211,6 +216,19 @@ def tile_probprotoseghead_t_kernel(tc, x, x_var, proto_mean, proto_var, out):
             nc.vector.tensor_reduce(out=s_all[:, 2 * g:2 * g + 1], in_=accs[g][:, 2, :],
                                     axis=mybir.AxisListType.X, op=ALU.add)
 
+        def copy_raw(g):
+            raws[g] = rpool.tile([P, 2, 2 * P], F32, name="raw")
+            copy = nc.vector.tensor_copy if vector_raw(g) else nc.scalar.copy
+            copy(out=raws[g][:], in_=banks[g][1][:])
+
+        def raw_sums(g):
+            raw = raws[g][:].bitcast(BF16).rearrange("q u (n e) -> q u n e", e=2)
+            for j in range(2):
+                for u in range(2):
+                    for e in range(2):
+                        nc.tensor.matmul(out=accs[g][:, 2, j:j + 1], lhsT=raw[:, u, j * P:(j + 1) * P, e],
+                                         rhs=neg_col[:], start=(u + e == 0), stop=(u + e == 2))
+
         def combine(g):
             c, t0 = where(g)
             acc = accs[g]
@@ -219,40 +237,61 @@ def tile_probprotoseghead_t_kernel(tc, x, x_var, proto_mean, proto_var, out):
             o_sb = o_tiles[c]
             for j in range(2):
                 nc.vector.scalar_tensor_tensor(out=o_sb[:, (t0 + j) * CM:(t0 + j + 1) * CM],
-                                               in0=acc[:, j, :], scalar=s_all[:, 2 * g + j:2 * g + j + 1],
+                                               in0=acc[:, j, :],
+                                               scalar=acc[:, 2, j:j + 1] if raw_v(g) else s_all[:, 2 * g + j:2 * g + j + 1],
                                                in1=bias_cm[:], op0=ALU.add, op1=ALU.add)
             if c == N_CHUNKS - 1:
                 nc.sync.dma_start(out=oc[c][:, t0 * CM:(t0 + 2) * CM], in_=o_sb[:, t0 * CM:(t0 + 2) * CM])
             elif t0 == T - 2:
                 nc.sync.dma_start(out=oc[c], in_=o_sb[:])
 
-        for i in range(N_GROUPS + 3):
-            q = i - 2
-            if i < N_GROUPS:
-                transposes(i)
-                grouped[i] = gpool.tile([P, 2048], BF16, name="gr", align_bytes=64)
-                if not vector_x(i):
-                    evacuate_x(i)
-                evacuate_v(i)
-            if 0 <= q < N_GROUPS:
-                accs[q] = psum_a.tile([P, 4, P], F32, name="acc")
-            if 0 <= q < N_GROUPS and pe_sums(q):
-                matmul_sums(q)
-            if 0 <= q < N_GROUPS:
-                quantise(q)
-            if 0 <= q < N_GROUPS:
-                multiply(q)
-            if 0 <= q - 1 < N_GROUPS:
-                combine(q - 1)
-            if 0 <= q < N_GROUPS and pe_sums(q):
-                reduce_sums(q)
-            if 0 <= i - 0 < N_GROUPS and vector_x(i - 0):
-                evacuate_x(i - 0)
-            if 0 <= i + 0 < N_GROUPS:
-                row_sums(i + 0)
+        for i in range(N_GROUPS + 4):
+            g = i - 0
+            if 0 <= g < N_GROUPS:
+                transposes(g)
+                grouped[g] = gpool.tile([P, 2048], BF16, name="gr", align_bytes=64)
+            g = i - 0
+            if 0 <= g < N_GROUPS and not vector_x(g):
+                evacuate_x(g)
+            g = i - 0
+            if 0 <= g < N_GROUPS:
+                if raw_v(g):
+                    copy_raw(g)
+                else:
+                    evacuate_v(g)
+            g = i - 0
+            if 0 <= g < N_GROUPS and raw_v(g):
+                evacuate_v(g)
+            g = i - 3
+            if 0 <= g < N_GROUPS:
+                accs[g] = psum_a.tile([P, 4, P], F32, name="acc")
+            g = i - 3
+            if 0 <= g < N_GROUPS and pe_sums(g):
+                matmul_sums(g)
+            g = i - 3
+            if 0 <= g < N_GROUPS:
+                multiply(g)
+            g = i - 4
+            if 0 <= g < N_GROUPS and pe_sums(g):
+                reduce_sums(g)
+            g = i - 2
+            if 0 <= g < N_GROUPS:
+                quantise(g)
+            g = i - 4
+            if 0 <= g < N_GROUPS:
+                combine(g)
+            g = i - 0
+            if 0 <= g < N_GROUPS and vector_x(g):
+                evacuate_x(g)
+            g = i - 0
+            if 0 <= g < N_GROUPS:
+                row_sums(g)
             if i == 0:
                 prototypes()
             if i == 1:
+                prototypes_scale()
+            if i == 2:
+                prototypes_quantise()
                 bias_row()
             if i < N_GROUPS:
                 c, t0 = where(i)

@@ -18,26 +18,29 @@ CM = 128
 LAMDA = 0.00390625
 T = 8
 N_CHUNKS = N_ROWS // (P * T)
-GROUPS_PER_CHUNK = T // 2
-N_GROUPS = N_CHUNKS * GROUPS_PER_CHUNK
+N_TILES = N_CHUNKS * T
+FIRST, LAST = 0, 0
+GROUPS = ([(r, 1) for r in range(FIRST)] + [(r, 2) for r in range(FIRST, N_TILES - LAST, 2)]
+          + [(r, 1) for r in range(N_TILES - LAST, N_TILES)])
+N_GROUPS = len(GROUPS)
 X_BUFS = 4
 S_COLS = 128
 
 
 def pe_sums(g):
-    return g % 5 in (1, 4)
+    return g % 5 == 4 or g % 10 == 2
 
 
 def raw_v(g):
-    return False
+    return g % 5 in (0, 1, 3)
 
 
 def vector_x(g):
-    return g % 11 == 5
+    return g % 10 == 4
 
 
 def vector_raw(g):
-    return False
+    return True
 
 
 FLOPS = 2 * 2 * N_ROWS * D * CM
@@ -56,7 +59,7 @@ def tile_probprotoseghead_t_kernel(tc, x, x_var, proto_mean, proto_var, out):
         gpool = ctx.enter_context(tc.tile_pool(name="gpool", bufs=6))
         cpool = ctx.enter_context(tc.tile_pool(name="cpool", bufs=5))
         jpool = ctx.enter_context(tc.tile_pool(name="jpool", bufs=2))
-        rpool = ctx.enter_context(tc.tile_pool(name="rpool", bufs=2))
+        rpool = ctx.enter_context(tc.tile_pool(name="rpool", bufs=5))
         opool = ctx.enter_context(tc.tile_pool(name="opool", bufs=3))
         psum_t = ctx.enter_context(tc.psum_pool(name="psum_t", bufs=3))
         psum_a = ctx.enter_context(tc.psum_pool(name="psum_a", bufs=2))
@@ -91,7 +94,7 @@ def tile_probprotoseghead_t_kernel(tc, x, x_var, proto_mean, proto_var, out):
         zeros = consts.tile([P, P], F32)
         nc.vector.memset(zeros[:], 0.0)
 
-        s_all = consts.tile([P, N_GROUPS * 2], F32)
+        s_all = consts.tile([P, N_TILES], F32)
         bias_cm = consts.tile([P, CM], F32)
         p_grouped = consts.tile([P, 2 * 4 * CM], BF16, align_bytes=64)
         neg_col = consts.tile([P, 1], BF16)
@@ -145,49 +148,53 @@ def tile_probprotoseghead_t_kernel(tc, x, x_var, proto_mean, proto_var, out):
             nc.vector.tensor_copy(out=bias_cm[:], in_=b_t[:, 0, :])
 
         def where(g):
-            return g // GROUPS_PER_CHUNK, 2 * (g % GROUPS_PER_CHUNK)
+            r, n = GROUPS[g]
+            return r // T, r % T, n
 
         def transposes(g):
-            c, t0 = where(g)
+            c, t0, n = where(g)
             xt = psum_t.tile([P, 2, 2 * P], F32, name="xt")
             vt = psum_t.tile([P, 2, 2 * P], F32, name="vt")
             banks[g] = (xt, vt)
+            grouped[g] = gpool.tile([P, 2048], BF16, name="gr", align_bytes=64)
             for src, dst in ((x_tiles[c], xt), (v_tiles[c], vt)):
                 words = src[:].bitcast(F32)
                 for u in range(2):
-                    for j in range(2):
+                    for j in range(n):
                         w0 = (t0 + j) * (D // 2) + u * P
                         nc.tensor.transpose(dst[:, u, j * P:(j + 1) * P], words[:, w0:w0 + P], ident[:])
 
         def evacuate_x(g):
-            dst = grouped[g][:, 0:1024].bitcast(F32).rearrange("q (n u) -> q n u", u=2)
-            src = banks[g][0][:].rearrange("q u n -> q n u")
+            c, t0, n = where(g)
+            dst = grouped[g][:, 0:512 * n].bitcast(F32).rearrange("q (n u) -> q n u", u=2)
+            src = banks[g][0][:, :, 0:n * P].rearrange("q u n -> q n u")
             if vector_x(g):
                 nc.vector.tensor_copy(out=dst, in_=src)
             else:
                 nc.scalar.copy(out=dst, in_=src)
 
         def evacuate_v(g):
-            vt = banks[g][1]
-            gr = grouped[g]
-            src = raws[g] if raw_v(g) else vt
-            nc.scalar.activation(out=gr[:, 1024:2048].rearrange("q (n u e) -> q n u e", u=2, e=2),
-                                 in_=src[:].bitcast(BF16).rearrange("q u (n e) -> q n u e", e=2),
+            c, t0, n = where(g)
+            src = raws[g] if raw_v(g) else banks[g][1]
+            nc.scalar.activation(out=grouped[g][:, 512 * n:1024 * n].rearrange("q (n u e) -> q n u e", u=2, e=2),
+                                 in_=src[:].bitcast(BF16)[:, :, 0:2 * n * P].rearrange("q u (n e) -> q n u e", e=2),
                                  func=ACTF.Sqrt)
 
         def quantise(g):
-            gr = grouped[g]
+            c, t0, n = where(g)
             cd = cpool.tile([P, 512], U32, name="cd", align_bytes=64)
             pl = cpool.tile([P, 512], U8, name="pl", align_bytes=64)
             codes[g] = (cd, pl)
-            nc.vector.quantize_mx(out=cd[:].bitcast(FP8X4), scales=pl[:], in_=gr[:])
+            nc.vector.quantize_mx(out=cd[:, 0:256 * n].bitcast(FP8X4), scales=pl[:, 0:256 * n],
+                                  in_=grouped[g][:, 0:1024 * n])
 
         def multiply(g):
             cd, pl = codes[g]
             acc = accs[g]
-            for j in range(2):
+            c, t0, n = where(g)
+            for j in range(n):
                 for h in range(2):
-                    cols = slice(h * 256 + j * P, h * 256 + (j + 1) * P)
+                    cols = slice((h * n + j) * P, (h * n + j + 1) * P)
                     pcols = slice(h * CM, (h + 1) * CM)
                     nc.tensor.matmul_mx(out=acc[:, j, :],
                                         lhsT=cd[:, cols].bitcast(FP8X4), lhsT_scale=pl[:, cols],
@@ -195,17 +202,17 @@ def tile_probprotoseghead_t_kernel(tc, x, x_var, proto_mean, proto_var, out):
                                         start=(h == 0), stop=(h == 1))
 
         def row_sums(g):
-            c, t0 = where(g)
-            for j in range(2):
+            c, t0, n = where(g)
+            for j in range(n):
                 if raw_v(g) or (j == 0 and pe_sums(g)):
                     continue
                 junk = jpool.tile([P, D], BF16, name="junk")
                 nc.vector.tensor_scalar(out=junk[:], in0=v_tiles[c][:, (t0 + j) * D:(t0 + j + 1) * D],
                                         scalar1=-LAMDA, scalar2=None, op0=ALU.mult, op1=ALU.add,
-                                        accum_out=s_all[:, 2 * g + j:2 * g + j + 1])
+                                        accum_out=s_all[:, c * T + t0 + j:c * T + t0 + j + 1])
 
         def matmul_sums(g):
-            c, t0 = where(g)
+            c, t0, n = where(g)
             parts = D // S_COLS
             for u in range(parts):
                 lo = t0 * D + u * S_COLS
@@ -213,7 +220,8 @@ def tile_probprotoseghead_t_kernel(tc, x, x_var, proto_mean, proto_var, out):
                                  start=(u == 0), stop=(u == parts - 1))
 
         def reduce_sums(g):
-            nc.vector.tensor_reduce(out=s_all[:, 2 * g:2 * g + 1], in_=accs[g][:, 2, :],
+            c, t0, n = where(g)
+            nc.vector.tensor_reduce(out=s_all[:, c * T + t0:c * T + t0 + 1], in_=accs[g][:, 2, :],
                                     axis=mybir.AxisListType.X, op=ALU.add)
 
         def copy_raw(g):
@@ -223,63 +231,69 @@ def tile_probprotoseghead_t_kernel(tc, x, x_var, proto_mean, proto_var, out):
 
         def raw_sums(g):
             raw = raws[g][:].bitcast(BF16).rearrange("q u (n e) -> q u n e", e=2)
-            for j in range(2):
+            c, t0, n = where(g)
+            for j in range(n):
                 for u in range(2):
                     for e in range(2):
                         nc.tensor.matmul(out=accs[g][:, 2, j:j + 1], lhsT=raw[:, u, j * P:(j + 1) * P, e],
                                          rhs=neg_col[:], start=(u + e == 0), stop=(u + e == 2))
 
         def combine(g):
-            c, t0 = where(g)
+            c, t0, n = where(g)
             acc = accs[g]
             if t0 == 0:
                 o_tiles[c] = opool.tile([P, T * CM], F32, name="o_sb")
             o_sb = o_tiles[c]
-            for j in range(2):
+            for j in range(n):
                 nc.vector.scalar_tensor_tensor(out=o_sb[:, (t0 + j) * CM:(t0 + j + 1) * CM],
                                                in0=acc[:, j, :],
-                                               scalar=acc[:, 2, j:j + 1] if raw_v(g) else s_all[:, 2 * g + j:2 * g + j + 1],
+                                               scalar=acc[:, 2, j:j + 1] if raw_v(g) else s_all[:, c * T + t0 + j:c * T + t0 + j + 1],
                                                in1=bias_cm[:], op0=ALU.add, op1=ALU.add)
             if c == N_CHUNKS - 1:
-                nc.sync.dma_start(out=oc[c][:, t0 * CM:(t0 + 2) * CM], in_=o_sb[:, t0 * CM:(t0 + 2) * CM])
-            elif t0 == T - 2:
+                nc.sync.dma_start(out=oc[c][:, t0 * CM:(t0 + n) * CM], in_=o_sb[:, t0 * CM:(t0 + n) * CM])
+            elif t0 + n == T:
                 nc.sync.dma_start(out=oc[c], in_=o_sb[:])
 
-        for i in range(N_GROUPS + 4):
+        for i in range(N_GROUPS + 5):
             g = i - 0
             if 0 <= g < N_GROUPS:
                 transposes(g)
-                grouped[g] = gpool.tile([P, 2048], BF16, name="gr", align_bytes=64)
+            g = i - 4
+            if 0 <= g < N_GROUPS:
+                accs[g] = psum_a.tile([P, 4, P], F32, name="acc")
+            g = i - 4
+            if 0 <= g < N_GROUPS and pe_sums(g):
+                matmul_sums(g)
+            g = i - 4
+            if 0 <= g < N_GROUPS and raw_v(g):
+                raw_sums(g)
+            g = i - 4
+            if 0 <= g < N_GROUPS:
+                multiply(g)
+            g = i - 1
+            if 0 <= g < N_GROUPS and raw_v(g):
+                evacuate_v(g)
             g = i - 0
             if 0 <= g < N_GROUPS and not vector_x(g):
                 evacuate_x(g)
             g = i - 0
-            if 0 <= g < N_GROUPS:
-                if raw_v(g):
-                    copy_raw(g)
-                else:
-                    evacuate_v(g)
+            if 0 <= g < N_GROUPS and raw_v(g) and not vector_raw(g):
+                copy_raw(g)
             g = i - 0
-            if 0 <= g < N_GROUPS and raw_v(g):
+            if 0 <= g < N_GROUPS and not raw_v(g):
                 evacuate_v(g)
-            g = i - 3
-            if 0 <= g < N_GROUPS:
-                accs[g] = psum_a.tile([P, 4, P], F32, name="acc")
-            g = i - 3
-            if 0 <= g < N_GROUPS and pe_sums(g):
-                matmul_sums(g)
-            g = i - 3
-            if 0 <= g < N_GROUPS:
-                multiply(g)
-            g = i - 4
+            g = i - 5
             if 0 <= g < N_GROUPS and pe_sums(g):
                 reduce_sums(g)
-            g = i - 2
+            g = i - 3
             if 0 <= g < N_GROUPS:
                 quantise(g)
-            g = i - 4
+            g = i - 5
             if 0 <= g < N_GROUPS:
                 combine(g)
+            g = i - 0
+            if 0 <= g < N_GROUPS and raw_v(g) and vector_raw(g):
+                copy_raw(g)
             g = i - 0
             if 0 <= g < N_GROUPS and vector_x(g):
                 evacuate_x(g)
@@ -294,6 +308,6 @@ def tile_probprotoseghead_t_kernel(tc, x, x_var, proto_mean, proto_var, out):
                 prototypes_quantise()
                 bias_row()
             if i < N_GROUPS:
-                c, t0 = where(i)
-                if t0 == T - 2 and c + X_BUFS < N_CHUNKS:
-                    load(c + X_BUFS, [(0, T)])
+                r, n = GROUPS[i]
+                if (r + n) % T == 0 and r // T + X_BUFS < N_CHUNKS:
+                    load(r // T + X_BUFS, [(0, T)])

@@ -56,13 +56,14 @@ def tile_probprotoseghead_t_kernel(tc, x, x_var, proto_mean, proto_var, out):
         ctx.enter_context(tc.manual_schedule())
         consts = ctx.enter_context(tc.tile_pool(name="consts", bufs=1))
         xpool = ctx.enter_context(tc.tile_pool(name="xpool", bufs=X_BUFS))
-        gpool = ctx.enter_context(tc.tile_pool(name="gpool", bufs=6))
-        cpool = ctx.enter_context(tc.tile_pool(name="cpool", bufs=5))
+        gpool = ctx.enter_context(tc.tile_pool(name="gpool", bufs=8))
+        cpool = ctx.enter_context(tc.tile_pool(name="cpool", bufs=6))
         jpool = ctx.enter_context(tc.tile_pool(name="jpool", bufs=2))
-        rpool = ctx.enter_context(tc.tile_pool(name="rpool", bufs=5))
-        opool = ctx.enter_context(tc.tile_pool(name="opool", bufs=3))
-        psum_t = ctx.enter_context(tc.psum_pool(name="psum_t", bufs=3))
-        psum_a = ctx.enter_context(tc.psum_pool(name="psum_a", bufs=2))
+        rpool = ctx.enter_context(tc.tile_pool(name="rpool", bufs=7))
+        opool = ctx.enter_context(tc.tile_pool(name="opool", bufs=5))
+        psum_x = ctx.enter_context(tc.psum_pool(name="psum_x", bufs=2))
+        psum_v = ctx.enter_context(tc.psum_pool(name="psum_v", bufs=3))
+        psum_a = ctx.enter_context(tc.psum_pool(name="psum_a", bufs=3))
 
         x_tiles = {}
         v_tiles = {}
@@ -114,8 +115,8 @@ def tile_probprotoseghead_t_kernel(tc, x, x_var, proto_mean, proto_var, out):
         o_tiles = {}
 
         def prototypes():
-            pm_t = psum_t.tile([P, 2, 2 * P], F32, name="xt")
-            pv_t = psum_t.tile([P, 2, 2 * P], F32, name="vt")
+            pm_t = psum_x.tile([P, 2, 2 * P], F32, name="xt")
+            pv_t = psum_v.tile([P, 2, 2 * P], F32, name="vt")
             for u in range(2):
                 nc.tensor.transpose(pm_t[:, u, 0:P], pm_sb[:].bitcast(F32)[:, u * P:(u + 1) * P], ident[:])
             for u in range(2):
@@ -153,8 +154,8 @@ def tile_probprotoseghead_t_kernel(tc, x, x_var, proto_mean, proto_var, out):
 
         def transposes(g):
             c, t0, n = where(g)
-            xt = psum_t.tile([P, 2, 2 * P], F32, name="xt")
-            vt = psum_t.tile([P, 2, 2 * P], F32, name="vt")
+            xt = psum_x.tile([P, 2, 2 * P], F32, name="xt")
+            vt = psum_v.tile([P, 2, 2 * P], F32, name="vt")
             banks[g] = (xt, vt)
             grouped[g] = gpool.tile([P, 2048], BF16, name="gr", align_bytes=64)
             for src, dst in ((x_tiles[c], xt), (v_tiles[c], vt)):
@@ -254,7 +255,7 @@ def tile_probprotoseghead_t_kernel(tc, x, x_var, proto_mean, proto_var, out):
             elif t0 + n == T:
                 nc.sync.dma_start(out=oc[c], in_=o_sb[:])
 
-        for i in range(N_GROUPS + 5):
+        for i in range(N_GROUPS + 6):
             g = i - 0
             if 0 <= g < N_GROUPS:
                 transposes(g)
@@ -282,13 +283,13 @@ def tile_probprotoseghead_t_kernel(tc, x, x_var, proto_mean, proto_var, out):
             g = i - 0
             if 0 <= g < N_GROUPS and not raw_v(g):
                 evacuate_v(g)
-            g = i - 5
+            g = i - 6
             if 0 <= g < N_GROUPS and pe_sums(g):
                 reduce_sums(g)
             g = i - 3
             if 0 <= g < N_GROUPS:
                 quantise(g)
-            g = i - 5
+            g = i - 6
             if 0 <= g < N_GROUPS:
                 combine(g)
             g = i - 0

from contextlib import ExitStack

import concourse.mybir as mybir
from concourse.masks import make_identity

F32 = mybir.dt.float32
BF16 = mybir.dt.bfloat16
U32 = mybir.dt.uint32
U8 = mybir.dt.uint8
FP8X4 = mybir.dt.float8_e4m3fn_x4
ALU = mybir.AluOpType
ACTF = mybir.ActivationFunctionType

P = 128
N_ROWS = 14336
D = 512
CM = 128
LAMDA = 0.00390625
T = 8
N_CHUNKS = N_ROWS // (P * T)
N_TILES = N_CHUNKS * T
FIRST, LAST = 0, 0
GROUPS = ([(r, 1) for r in range(FIRST)] + [(r, 2) for r in range(FIRST, N_TILES - LAST, 2)]
          + [(r, 1) for r in range(N_TILES - LAST, N_TILES)])
N_GROUPS = len(GROUPS)
X_BUFS = 4
S_COLS = 128


def pe_sums(g):
    return g % 5 == 4 or g % 10 == 2


def raw_v(g):
    return g % 5 in (0, 1, 3)


def vector_x(g):
    return g % 10 == 4


def vector_raw(g):
    return True


FLOPS = 2 * 2 * N_ROWS * D * CM


def tile_probprotoseghead_t_kernel(tc, x, x_var, proto_mean, proto_var, out):
    nc = tc.nc
    xc = x.rearrange("(c p t) d -> c p (t d)", p=P, t=T)
    vc = x_var.rearrange("(c p t) d -> c p (t d)", p=P, t=T)
    oc = out.rearrange("(c p t) a b -> c p (t a b)", p=P, t=T)

    with ExitStack() as ctx:
        ctx.enter_context(tc.manual_schedule())
        consts = ctx.enter_context(tc.tile_pool(name="consts", bufs=1))
        xpool = ctx.enter_context(tc.tile_pool(name="xpool", bufs=X_BUFS))
        gpool = ctx.enter_context(tc.tile_pool(name="gpool", bufs=8))
        cpool = ctx.enter_context(tc.tile_pool(name="cpool", bufs=6))
        jpool = ctx.enter_context(tc.tile_pool(name="jpool", bufs=2))
        rpool = ctx.enter_context(tc.tile_pool(name="rpool", bufs=7))
        opool = ctx.enter_context(tc.tile_pool(name="opool", bufs=5))
        psum_x = ctx.enter_context(tc.psum_pool(name="psum_x", bufs=2))
        psum_v = ctx.enter_context(tc.psum_pool(name="psum_v", bufs=3))
        psum_a = ctx.enter_context(tc.psum_pool(name="psum_a", bufs=3))

        x_tiles = {}
        v_tiles = {}

        def load(c, cuts):
            x_sb = xpool.tile([P, T * D], BF16, name="x_sb")
            v_sb = xpool.tile([P, T * D], BF16, name="v_sb")
            x_tiles[c] = x_sb
            v_tiles[c] = v_sb
            for lo, hi in cuts:
                nc.sync.dma_start(out=x_sb[:, lo * D:hi * D], in_=xc[c][:, lo * D:hi * D])
                nc.sync.dma_start(out=v_sb[:, lo * D:hi * D], in_=vc[c][:, lo * D:hi * D])

        pm_sb = consts.tile([P, D], BF16)
        pv_sb = consts.tile([P, D], BF16)
        nc.scalar.dma_start(out=pm_sb[:], in_=proto_mean.rearrange("c m d -> (c m) d"))
        nc.scalar.dma_start(out=pv_sb[:], in_=proto_var.rearrange("c m d -> (c m) d"))
        load(0, [(0, 2), (2, 4), (4, T)])
        load(1, [(0, 4), (4, T)])
        for c in range(2, X_BUFS):
            load(c, [(0, T)])

        ident = consts.tile([P, P], F32)
        make_identity(nc, ident[:])
        warm_in = consts.tile([P, 1], F32)
        warm_out = consts.tile([P, 1], F32)
        nc.vector.memset(warm_in[:], 1.0)
        nc.scalar.activation(out=warm_out[:], in_=warm_in[:], func=ACTF.Sqrt)
        zeros = consts.tile([P, P], F32)
        nc.vector.memset(zeros[:], 0.0)

        s_all = consts.tile([P, N_TILES], F32)
        bias_cm = consts.tile([P, CM], F32)
        p_grouped = consts.tile([P, 2 * 4 * CM], BF16, align_bytes=64)
        neg_col = consts.tile([P, 1], BF16)
        nc.vector.memset(neg_col[:], -LAMDA)
        neg_ident = consts.tile([P, P], BF16)
        p_codes = consts.tile([P, 2 * CM], U32, align_bytes=64)
        p_plane = consts.tile([P, 2 * CM], U8, align_bytes=64)
        p_sqrt = consts.tile([P, 4 * CM], F32)
        sp_neg = consts.tile([P, 1], F32)
        b_rep = consts.tile([P, P], F32)

        banks = {}
        grouped = {}
        codes = {}
        accs = {}
        raws = {}
        o_tiles = {}

        def prototypes():
            pm_t = psum_x.tile([P, 2, 2 * P], F32, name="xt")
            pv_t = psum_v.tile([P, 2, 2 * P], F32, name="vt")
            for u in range(2):
                nc.tensor.transpose(pm_t[:, u, 0:P], pm_sb[:].bitcast(F32)[:, u * P:(u + 1) * P], ident[:])
            for u in range(2):
                nc.tensor.transpose(pv_t[:, u, 0:P], pv_sb[:].bitcast(F32)[:, u * P:(u + 1) * P], ident[:])
            nc.vector.tensor_scalar(
                out=p_grouped[:, 0:4 * CM].rearrange("q (r u e) -> q r u e", u=2, e=2),
                in0=pm_t[:].bitcast(BF16)[:, :, 0:2 * P].rearrange("q u (r e) -> q r u e", e=2),
                scalar1=2.0, scalar2=None, op0=ALU.mult)
            nc.scalar.activation(
                out=p_sqrt[:].rearrange("q (r u e) -> q r u e", u=2, e=2),
                in_=pv_t[:].bitcast(BF16)[:, :, 0:2 * P].rearrange("q u (r e) -> q r u e", e=2),
                func=ACTF.Sqrt)
            junk0 = jpool.tile([P, D], BF16, name="junk")
            nc.vector.tensor_scalar(out=junk0[:], in0=pv_sb[:], scalar1=-LAMDA, scalar2=None,
                                    op0=ALU.mult, op1=ALU.add, accum_out=sp_neg[:])

        def prototypes_scale():
            nc.vector.tensor_scalar(out=b_rep[:], in0=zeros[:], scalar1=sp_neg[:, 0:1], scalar2=-2.0,
                                    op0=ALU.add, op1=ALU.add)
            nc.vector.tensor_scalar(out=p_grouped[:, 4 * CM:8 * CM], in0=p_sqrt[:],
                                    scalar1=2.0 * LAMDA, scalar2=None, op0=ALU.mult)

        def prototypes_quantise():
            nc.vector.quantize_mx(out=p_codes[:].bitcast(FP8X4), scales=p_plane[:], in_=p_grouped[:])
            nc.vector.tensor_scalar(out=neg_ident[:], in0=ident[:], scalar1=-LAMDA, scalar2=None, op0=ALU.mult)

        def bias_row():
            b_t = psum_a.tile([P, 4, P], F32, name="acc")
            nc.tensor.transpose(b_t[:, 0, :], b_rep[:], ident[:])
            nc.vector.tensor_copy(out=bias_cm[:], in_=b_t[:, 0, :])

        def where(g):
            r, n = GROUPS[g]
            return r // T, r % T, n

        def transposes(g):
            c, t0, n = where(g)
            xt = psum_x.tile([P, 2, 2 * P], F32, name="xt")
            vt = psum_v.tile([P, 2, 2 * P], F32, name="vt")
            banks[g] = (xt, vt)
            grouped[g] = gpool.tile([P, 2048], BF16, name="gr", align_bytes=64)
            for src, dst in ((x_tiles[c], xt), (v_tiles[c], vt)):
                words = src[:].bitcast(F32)
                for u in range(2):
                    for j in range(n):
                        w0 = (t0 + j) * (D // 2) + u * P
                        nc.tensor.transpose(dst[:, u, j * P:(j + 1) * P], words[:, w0:w0 + P], ident[:])

        def evacuate_x(g):
            c, t0, n = where(g)
            dst = grouped[g][:, 0:512 * n].bitcast(F32).rearrange("q (n u) -> q n u", u=2)
            src = banks[g][0][:, :, 0:n * P].rearrange("q u n -> q n u")
            if vector_x(g):
                nc.vector.tensor_copy(out=dst, in_=src)
            else:
                nc.scalar.copy(out=dst, in_=src)

        def evacuate_v(g):
            c, t0, n = where(g)
            src = raws[g] if raw_v(g) else banks[g][1]
            nc.scalar.activation(out=grouped[g][:, 512 * n:1024 * n].rearrange("q (n u e) -> q n u e", u=2, e=2),
                                 in_=src[:].bitcast(BF16)[:, :, 0:2 * n * P].rearrange("q u (n e) -> q n u e", e=2),
                                 func=ACTF.Sqrt)

        def quantise(g):
            c, t0, n = where(g)
            cd = cpool.tile([P, 512], U32, name="cd", align_bytes=64)
            pl = cpool.tile([P, 512], U8, name="pl", align_bytes=64)
            codes[g] = (cd, pl)
            nc.vector.quantize_mx(out=cd[:, 0:256 * n].bitcast(FP8X4), scales=pl[:, 0:256 * n],
                                  in_=grouped[g][:, 0:1024 * n])

        def multiply(g):
            cd, pl = codes[g]
            acc = accs[g]
            c, t0, n = where(g)
            for j in range(n):
                for h in range(2):
                    cols = slice((h * n + j) * P, (h * n + j + 1) * P)
                    pcols = slice(h * CM, (h + 1) * CM)
                    nc.tensor.matmul_mx(out=acc[:, j, :],
                                        lhsT=cd[:, cols].bitcast(FP8X4), lhsT_scale=pl[:, cols],
                                        rhs=p_codes[:, pcols].bitcast(FP8X4), rhs_scale=p_plane[:, pcols],
                                        start=(h == 0), stop=(h == 1))

        def row_sums(g):
            c, t0, n = where(g)
            for j in range(n):
                if raw_v(g) or (j == 0 and pe_sums(g)):
                    continue
                junk = jpool.tile([P, D], BF16, name="junk")
                nc.vector.tensor_scalar(out=junk[:], in0=v_tiles[c][:, (t0 + j) * D:(t0 + j + 1) * D],
                                        scalar1=-LAMDA, scalar2=None, op0=ALU.mult, op1=ALU.add,
                                        accum_out=s_all[:, c * T + t0 + j:c * T + t0 + j + 1])

        def matmul_sums(g):
            c, t0, n = where(g)
            parts = D // S_COLS
            for u in range(parts):
                lo = t0 * D + u * S_COLS
                nc.tensor.matmul(out=accs[g][:, 2, :], lhsT=neg_ident[:], rhs=v_tiles[c][:, lo:lo + S_COLS],
                                 start=(u == 0), stop=(u == parts - 1))

        def reduce_sums(g):
            c, t0, n = where(g)
            nc.vector.tensor_reduce(out=s_all[:, c * T + t0:c * T + t0 + 1], in_=accs[g][:, 2, :],
                                    axis=mybir.AxisListType.X, op=ALU.add)

        def copy_raw(g):
            raws[g] = rpool.tile([P, 2, 2 * P], F32, name="raw")
            copy = nc.vector.tensor_copy if vector_raw(g) else nc.scalar.copy
            copy(out=raws[g][:], in_=banks[g][1][:])

        def raw_sums(g):
            raw = raws[g][:].bitcast(BF16).rearrange("q u (n e) -> q u n e", e=2)
            c, t0, n = where(g)
            for j in range(n):
                for u in range(2):
                    for e in range(2):
                        nc.tensor.matmul(out=accs[g][:, 2, j:j + 1], lhsT=raw[:, u, j * P:(j + 1) * P, e],
                                         rhs=neg_col[:], start=(u + e == 0), stop=(u + e == 2))

        def combine(g):
            c, t0, n = where(g)
            acc = accs[g]
            if t0 == 0:
                o_tiles[c] = opool.tile([P, T * CM], F32, name="o_sb")
            o_sb = o_tiles[c]
            for j in range(n):
                nc.vector.scalar_tensor_tensor(out=o_sb[:, (t0 + j) * CM:(t0 + j + 1) * CM],
                                               in0=acc[:, j, :],
                                               scalar=acc[:, 2, j:j + 1] if raw_v(g) else s_all[:, c * T + t0 + j:c * T + t0 + j + 1],
                                               in1=bias_cm[:], op0=ALU.add, op1=ALU.add)
            if c == N_CHUNKS - 1:
                nc.sync.dma_start(out=oc[c][:, t0 * CM:(t0 + n) * CM], in_=o_sb[:, t0 * CM:(t0 + n) * CM])
            elif t0 + n == T:
                nc.sync.dma_start(out=oc[c], in_=o_sb[:])

        for i in range(N_GROUPS + 6):
            g = i - 0
            if 0 <= g < N_GROUPS:
                transposes(g)
            g = i - 4
            if 0 <= g < N_GROUPS:
                accs[g] = psum_a.tile([P, 4, P], F32, name="acc")
            g = i - 4
            if 0 <= g < N_GROUPS and pe_sums(g):
                matmul_sums(g)
            g = i - 4
            if 0 <= g < N_GROUPS and raw_v(g):
                raw_sums(g)
            g = i - 4
            if 0 <= g < N_GROUPS:
                multiply(g)
            g = i - 1
            if 0 <= g < N_GROUPS and raw_v(g):
                evacuate_v(g)
            g = i - 0
            if 0 <= g < N_GROUPS and not vector_x(g):
                evacuate_x(g)
            g = i - 0
            if 0 <= g < N_GROUPS and raw_v(g) and not vector_raw(g):
                copy_raw(g)
            g = i - 0
            if 0 <= g < N_GROUPS and not raw_v(g):
                evacuate_v(g)
            g = i - 6
            if 0 <= g < N_GROUPS and pe_sums(g):
                reduce_sums(g)
            g = i - 3
            if 0 <= g < N_GROUPS:
                quantise(g)
            g = i - 6
            if 0 <= g < N_GROUPS:
                combine(g)
            g = i - 0
            if 0 <= g < N_GROUPS and raw_v(g) and vector_raw(g):
                copy_raw(g)
            g = i - 0
            if 0 <= g < N_GROUPS and vector_x(g):
                evacuate_x(g)
            g = i - 0
            if 0 <= g < N_GROUPS:
                row_sums(g)
            if i == 0:
                prototypes()
            if i == 1:
                prototypes_scale()
            if i == 2:
                prototypes_quantise()
                bias_row()
            if i < N_GROUPS:
                r, n = GROUPS[i]
                if (r + n) % T == 0 and r // T + X_BUFS < N_CHUNKS:
                    load(r // T + X_BUFS, [(0, T)])
